import numpy as np
import ml_dtypes


def mxq(x, axis, fmt="e4m3"):
    dtype, down = {"e4m3": (ml_dtypes.float8_e4m3fn, 7), "e5m2": (ml_dtypes.float8_e5m2, 14)}[fmt]
    v = np.moveaxis(np.asarray(x, np.float32).astype(ml_dtypes.bfloat16).astype(np.float64), axis, -1)
    blocks = v.reshape(v.shape[:-1] + (-1, 32))
    amax = np.abs(blocks).max(-1, keepdims=True)
    byte = np.maximum(np.where(amax > 0, np.frexp(amax)[1] - 1 + 127, 0) - down, 1)
    scale = np.exp2(byte - 127.0)
    codes = (blocks / scale).astype(np.float32).astype(dtype).astype(np.float64)
    return np.moveaxis((codes * scale).reshape(v.shape), -1, axis)


WIDE = False


def mx_kscale(k):
    if not WIDE:
        return np.ones(k)
    levels = np.array([18, -18])
    if k % 512:
        return np.exp2(np.random.permutation(np.resize(levels, k // 32))).repeat(32)
    a = np.empty((k // 512, 16))
    for p in range(k // 512):
        a[p, :8] = np.random.permutation(np.resize(levels, 8))
        for g in range(8):
            far = levels[np.abs(levels - a[p, g]) >= 10]
            a[p, g + 8] = far[np.random.randint(len(far))]
    return np.exp2(a.ravel()).repeat(32)


BF16 = ml_dtypes.bfloat16


def bf(x):
    return np.asarray(x, np.float32).astype(BF16)


def f64(x):
    return np.asarray(x).astype(np.float64)


B, N_IN, N_UNITS, N_EXC = 1024, 512, 2048, 1024


def setup_inputs():
    s = mx_kscale(B)[:, None]
    u_exc = mx_kscale(N_EXC)
    u_inh = mx_kscale(N_UNITS - N_EXC)
    u = np.concatenate([u_exc, u_inh])
    x0 = bf(np.random.standard_normal((B, N_IN)))
    y_exc = bf(np.random.random((B, N_EXC)))
    s_exc = bf(np.random.random((B, N_EXC)))
    y_inh = bf(np.random.random((B, N_EXC)))
    s_inh = bf(np.random.random((B, N_EXC)))
    w0 = bf(np.random.standard_normal((N_IN, N_UNITS)) / np.sqrt(N_IN))
    eiw = bf(np.random.standard_normal((N_EXC, N_EXC)) / np.sqrt(N_EXC))
    l = bf(np.random.standard_normal(N_UNITS) * 0.5)
    xw = f64(x0) @ f64(w0)
    z_exc = xw[:, :N_EXC] + f64(y_exc) + f64(y_inh) @ f64(eiw) + f64(l)[:N_EXC] * f64(s_exc) * (1.0 - f64(y_exc))
    z_inh = xw[:, N_EXC:] + f64(y_inh) - f64(y_exc) @ f64(eiw).T + f64(l)[N_EXC:] * f64(s_inh) * (1.0 - f64(y_inh))
    g0 = np.random.standard_normal((B, N_EXC)) * np.exp2(np.random.randint(-6, 1, (B, 1)))
    g1 = np.random.standard_normal((B, N_EXC)) * np.exp2(np.random.randint(-6, 1, (B, 1)))
    g0 = np.where(np.abs(z_exc) < 1e-3, 0.0, g0)
    g1 = np.where(np.abs(z_inh) < 1e-3, 0.0, g1)
    return {
        "x_t": bf(f64(x0) * s),
        "y_exc": y_exc,
        "s_exc": s_exc,
        "y_inh": y_inh,
        "s_inh": s_inh,
        "iw": bf(f64(w0) / u),
        "eiw": eiw,
        "l": l,
        "z_exc": np.asarray(z_exc, np.float32),
        "z_inh": np.asarray(z_inh, np.float32),
        "grad_0": bf(g0 / s * u_exc),
        "grad_1": bf(g1 / s * u_inh),
    }


def reference(x_t, y_exc, s_exc, y_inh, s_inh, iw, eiw, l, z_exc, z_inh, grad_0, grad_1):
    dz_exc = np.where(f64(z_exc) > 0.0, f64(grad_0), 0.0)
    dz_inh = np.where(f64(z_inh) > 0.0, f64(grad_1), 0.0)
    dz = np.concatenate([dz_exc, dz_inh], axis=1)
    dx = mxq(dz, 1, "e5m2") @ mxq(f64(iw), 1, "e4m3").T
    diw = mxq(f64(x_t), 0, "e4m3").T @ mxq(dz, 0, "e5m2")
    return dx, diw

@@ -1,0 +1,392 @@
+from contextlib import ExitStack
+
+import concourse.mybir as mybir
+from concourse.masks import make_identity
+
+TOKENS, N_IN, UNITS, HALF = 1024, 512, 2048, 1024
+FLOPS = 2 * (2 * TOKENS * UNITS * N_IN)
+BYTES = 2 * TOKENS * N_IN + 2 * N_IN * UNITS + 6 * TOKENS * UNITS + 4 * TOKENS * N_IN + 4 * N_IN * UNITS
+
+F32 = mybir.dt.float32
+BF16 = mybir.dt.bfloat16
+U32 = mybir.dt.uint32
+U8 = mybir.dt.uint8
+E4M3 = mybir.dt.float8_e4m3fn_x4
+E5M2 = mybir.dt.float8_e5m2_x4
+ALU = mybir.AluOpType
+
+P = 128
+W = 512
+GROUPS = TOKENS // W
+CHUNKS = UNITS // W
+BLOCKS = [[0,0],[0,1],[1,0],[1,1],[0,3],[0,2],[1,2],[1,3]]
+SPLITS = [320,384,320,256,192,320,0,512]
+XSPLITS = [256,0]
+LOADS = [["b",0],["w",0],["b",2],["b",3],["x",1],["x",0],["b",1],["w",3],["w",1],["b",5],["b",4],["w",2],["b",6],["b",7]]
+ORDER = [
+    ["A",0,0],
+    ["T",0,0],
+    ["A",0,1],
+    ["E",0,0],
+    ["LS",0],
+    ["T",0,1],
+    ["LV",0],
+    ["TI",0,0],
+    ["E",0,1],
+    ["QT",0],
+    ["TI",0,1],
+    ["EI",0,0],
+    ["QU",0],
+    ["EI",0,1],
+    ["IQ",0],
+    ["A",2,0],
+    ["M0",0,0],
+    ["A",2,1],
+    ["T",2,0],
+    ["E",2,0],
+    ["T",2,1],
+    ["LV",2],
+    ["LS",2],
+    ["A",3,0],
+    ["E",2,1],
+    ["QU",2],
+    ["XS",1],
+    ["T",3,0],
+    ["A",3,1],
+    ["XV",0],
+    ["T",3,1],
+    ["QT",2],
+    ["E",3,0],
+    ["XQ",1],
+    ["E",3,1],
+    ["LV",3],
+    ["LS",3],
+    ["QU",3],
+    ["A",1,0],
+    ["XS",0],
+    ["TI",3,0],
+    ["A",1,1],
+    ["T",1,0],
+    ["EI",3,0],
+    ["TI",1,0],
+    ["E",1,0],
+    ["XQ",0],
+    ["T",1,1],
+    ["EI",1,0],
+    ["QT",3],
+    ["TI",1,1],
+    ["E",1,1],
+    ["LV",1],
+    ["TI",3,1],
+    ["EI",1,1],
+    ["P1",0,0],
+    ["EI",3,1],
+    ["QU",1],
+    ["M1",0,0],
+    ["P1",0,1],
+    ["C1",0,0,"S"],
+    ["IQ",1],
+    ["M1",0,1],
+    ["P1",0,2],
+    ["C1",0,1,"S"],
+    ["A",5,0],
+    ["M1",0,2],
+    ["M0",0,1],
+    ["C1",0,2,"S"],
+    ["A",5,1],
+    ["LS",1],
+    ["T",5,0],
+    ["QT",1],
+    ["T",5,1],
+    ["E",5,0],
+    ["IQ",3],
+    ["P1",0,3],
+    ["E",5,1],
+    ["M1",0,3],
+    ["A",4,0],
+    ["LS",5],
+    ["P1",1,0],
+    ["M1",1,0],
+    ["P1",1,1],
+    ["M1",1,1],
+    ["C1",0,3,"S"],
+    ["C1",1,0,"V"],
+    ["TI",2,0],
+    ["C1",1,1,"S"],
+    ["A",4,1],
+    ["TI",2,1],
+    ["EI",2,0],
+    ["T",4,0],
+    ["EI",2,1],
+    ["QU",5],
+    ["T",4,1],
+    ["E",4,0],
+    ["IQ",2],
+    ["P1",1,2],
+    ["E",4,1],
+    ["LV",4],
+    ["M1",1,2],
+    ["M0",0,2],
+    ["C1",1,2,"S"],
+    ["QU",4],
+    ["LS",4],
+    ["A",6,0],
+    ["M0",0,3],
+    ["A",6,1],
+    ["T",6,0],
+    ["C0",0,0,"S"],
+    ["C0",0,1,"S"],
+    ["C0",0,2,"V"],
+    ["T",6,1],
+    ["C0",0,3,"S"],
+    ["A",7,0],
+    ["P1",1,3],
+    ["E",6,0],
+    ["M1",1,3],
+    ["M0",1,0],
+    ["C1",1,3,"S"],
+    ["A",7,1],
+    ["E",6,1],
+    ["M0",1,1],
+    ["LS",6],
+    ["QU",6],
+    ["QT",4],
+    ["M0",1,2],
+    ["LV",5],
+    ["T",7,0],
+    ["QT",5],
+    ["T",7,1],
+    ["E",7,0],
+    ["QT",6],
+    ["P1",2,0],
+    ["E",7,1],
+    ["LV",7],
+    ["M1",2,0],
+    ["P1",2,1],
+    ["C1",2,0,"S"],
+    ["M1",2,1],
+    ["P1",2,2],
+    ["C1",2,1,"S"],
+    ["QU",7],
+    ["M1",2,2],
+    ["P1",2,3],
+    ["C1",2,2,"S"],
+    ["QT",7],
+    ["M1",2,3],
+    ["M0",1,3],
+    ["C1",2,3,"S"],
+    ["M1",3,0],
+    ["C0",1,0,"V"],
+    ["C0",1,1,"S"],
+    ["M1",3,1],
+    ["C0",1,2,"S"],
+    ["C0",1,3,"V"],
+    ["M1",3,2],
+    ["C1",3,0,"S"],
+    ["C1",3,1,"V"],
+    ["M1",3,3],
+    ["C1",3,2,"V"],
+    ["C1",3,3,"V"],
+]
+
+
+def tile_eisnucell_pa_v_kernel(
+    tc, x_t, y_exc, s_exc, y_inh, s_inh, iw, eiw, l, z_exc, z_inh, grad_0, grad_1, out_0, out_1
+):
+    nc = tc.nc
+    with ExitStack() as ctx:
+        keep = ctx.enter_context(tc.tile_pool(name="keep", bufs=1))
+        zpool = ctx.enter_context(tc.tile_pool(name="zpool", bufs=5))
+        gpool = ctx.enter_context(tc.tile_pool(name="gpool", bufs=6))
+        rawpool = ctx.enter_context(tc.tile_pool(name="rawpool", bufs=6))
+        dzpool = ctx.enter_context(tc.tile_pool(name="dzpool", bufs=4))
+        lacepool = ctx.enter_context(tc.tile_pool(name="lacepool", bufs=4))
+        turnpool = ctx.enter_context(tc.tile_pool(name="turnpool", bufs=5))
+        out0pool = ctx.enter_context(tc.tile_pool(name="out0pool", bufs=2))
+        out1pool = ctx.enter_context(tc.tile_pool(name="out1pool", bufs=2))
+        psum = ctx.enter_context(tc.psum_pool(name="psum", bufs=4))
+        psum_sum = ctx.enter_context(tc.psum_pool(name="psum_sum", bufs=1))
+        ctx.enter_context(tc.manual_schedule())
+
+        ident = keep.tile([P, P], F32, name="ident")
+        make_identity(nc, ident[:])
+
+        blocks = BLOCKS
+        z_sb, g_sb, iw_sb, x_sb = {}, {}, {}, {}
+
+        def load_block(b, parts):
+            g, u = blocks[b]
+            z_hbm, g_hbm = (z_exc, grad_0) if u < CHUNKS // 2 else (z_inh, grad_1)
+            rows = slice(g * W, (g + 1) * W)
+            cols = slice(u * W % HALF, u * W % HALF + W)
+            g_view = g_hbm[rows, cols].rearrange("(p j) w -> p j w", j=4)
+            z_view = z_hbm[rows, cols].rearrange("(p j) w -> p j w", j=4)
+            gt = gpool.tile([P, 4, W], BF16, name="gt", tag="gt")
+            zt = zpool.tile([P, 4, W], F32, name="zt", tag="zt")
+            for i in range(parts):
+                js = slice(4 // parts * i, 4 // parts * (i + 1))
+                nc.sync.dma_start(out=gt[:, js, :], in_=g_view[:, js, :])
+                nc.sync.dma_start(out=zt[:, js, :], in_=z_view[:, js, :])
+            z_sb[b], g_sb[b] = zt, gt
+
+        def load_iw(u):
+            t = rawpool.tile([P, 4, W], BF16, name="raw", tag="raw")
+            nc.sync.dma_start(out=t[:], in_=iw[:, u * W : (u + 1) * W].rearrange("(r p) k -> p r k", p=P))
+            iw_sb[u] = t
+
+        def load_x(g):
+            t = rawpool.tile([P, 4, W], BF16, name="raw", tag="raw")
+            nc.sync.dma_start(out=t[:], in_=x_t[g * W : (g + 1) * W, :].rearrange("(p j) w -> p j w", j=4))
+            x_sb[g] = t
+
+        for kind, i in LOADS:
+            if kind == "b":
+                load_block(i, 2 if i == 0 else 1)
+            elif kind == "w":
+                load_iw(i)
+            else:
+                load_x(i)
+
+        sc, ve = nc.scalar.copy, nc.vector.tensor_copy
+
+        def lace(engine_copy, dst, src, c0, c1):
+            engine_copy(
+                out=dst[:, c0:c1, :].rearrange("p (c i) t -> p c t i", i=4),
+                in_=src[:, :, c0:c1].rearrange("p t (c i) -> p c t i", i=4),
+            )
+
+        def turn(src, h):
+            words = src[:].rearrange("p j w -> p (j w)").bitcast(F32)
+            bank = psum.tile([P, 2, 2, P], F32, name="bank", tag="bank")
+            for jj in range(2):
+                for e in range(2):
+                    j = 2 * h + jj
+                    nc.tensor.transpose(bank[:, jj, e, :], words[:, 256 * j + e : 256 * (j + 1) : 2], ident[:])
+            return bank
+
+        def unload_turn(bank, dst, h):
+            nc.scalar.copy(
+                out=dst[:].bitcast(F32)[:, 512 * h : 512 * (h + 1)].rearrange("p (j q u) -> p j q u", j=2, u=2),
+                in_=bank[:].rearrange("p j u q -> p j q u"),
+            )
+
+        def quantise(src2d, fmt, pool, tag):
+            codes = pool.tile([P, W], U32, name=tag + "_c", tag=tag + "_c", align_bytes=64)
+            scales = pool.tile([P, W], U8, name=tag + "_s", tag=tag + "_s", align_bytes=64)
+            nc.vector.quantize_mx(out=codes[:].bitcast(fmt), scales=scales[:], in_=src2d)
+            return codes, scales
+
+        def mm(out, left, lfmt, lcols, right, rfmt, start, stop):
+            nc.tensor.matmul_mx(
+                out=out,
+                lhsT=left[0][:, lcols].bitcast(lfmt),
+                lhsT_scale=left[1][:, lcols],
+                rhs=right[0][:].bitcast(rfmt),
+                rhs_scale=right[1][:],
+                start=start,
+                stop=stop,
+            )
+
+        def flat(t):
+            return t[:].rearrange("p w t -> p (w t)")
+
+        at = {tuple(blk): b for b, blk in enumerate(blocks)}
+        dz, laced, turned, banks = {}, {}, {}, {}
+        dz_tok, dz_unit, iw_codes, x_codes, sums, res0, res1 = {}, {}, {}, {}, {}, {}, {}
+        copy = {"V": nc.vector.tensor_copy, "S": nc.scalar.copy}
+
+        def mask(b, h):
+            if h == 0:
+                dz[b] = dzpool.tile([P, 4, W], BF16, name="dz", tag="dz")
+            js = slice(2 * h, 2 * h + 2)
+            nc.vector.scalar_tensor_tensor(
+                out=dz[b][:, js, :], in0=z_sb[b][:, js, :], scalar=0.0, in1=g_sb[b][:, js, :], op0=ALU.is_gt, op1=ALU.mult
+            )
+
+        def lace_part(key, src, e, c0, c1):
+            if key not in laced:
+                laced[key] = lacepool.tile([P, W, 4], BF16, name="laced", tag="laced", align_bytes=64)
+            lace(copy[e], laced[key], src, c0, c1)
+
+        def unload(key, h):
+            if key not in turned:
+                turned[key] = turnpool.tile([P, 4 * W], BF16, name="turned", tag="turned", align_bytes=64)
+            unload_turn(banks[key + (h,)], turned[key], h)
+
+        def products0(g, u):
+            for j in range(4):
+                if u == 0:
+                    sums[(g, j)] = psum_sum.tile([P, W], F32, name="sum0_%d" % j, tag="sum0_%d" % j)
+                mm(
+                    sums[(g, j)][:], dz_unit[at[(g, u)]], E5M2, slice(P * j, P * (j + 1)), iw_codes[u], E4M3,
+                    u == 0, u == CHUNKS - 1,
+                )
+
+        def pass1(u, m, g):
+            if g == 0:
+                banks[("m", u, m)] = psum.tile([P, W], F32, name="bank", tag="bank")
+            mm(
+                banks[("m", u, m)][:], x_codes[g], E4M3, slice(P * m, P * (m + 1)), dz_tok[at[(g, u)]], E5M2,
+                g == 0, g == GROUPS - 1,
+            )
+
+        done = set()
+
+        def store(res, view, key, j, e, src):
+            copy[e](out=res[:, j, :], in_=src[:])
+            done.add(key + (j,))
+            if key + (j ^ 1,) in done:
+                js = slice(j // 2 * 2, j // 2 * 2 + 2)
+                nc.sync.dma_start(out=view[:, js, :], in_=res[:, js, :])
+
+        def copy0(g, j, e):
+            if g not in res0:
+                res0[g] = out0pool.tile([P, 4, W], F32, name="res0", tag="res0")
+            store(res0[g], out_0[g * W : (g + 1) * W, :].rearrange("(p j) n -> p j n", j=4), (0, g), j, e, sums[(g, j)])
+
+        def copy1(u, m, e):
+            if u not in res1:
+                res1[u] = out1pool.tile([P, 4, W], F32, name="res1", tag="res1")
+            store(res1[u], out_1[:, u * W : (u + 1) * W].rearrange("(m p) n -> p m n", p=P), (1, u), m, e, banks[("m", u, m)])
+
+        early = {(s[1], s[2]) for s in ORDER if s[0] == "P1"}
+        for s in ORDER:
+            k, i = s[0], s[1]
+            if k == "A":
+                mask(i, s[2])
+            elif k == "T":
+                banks[("t", i, s[2])] = turn(dz[i], s[2])
+            elif k == "E":
+                unload(("t", i), s[2])
+            elif k == "TI":
+                banks[("w", i, s[2])] = turn(iw_sb[i], s[2])
+            elif k == "EI":
+                unload(("w", i), s[2])
+            elif k == "LV":
+                lace_part(("t", i), dz[i], "V", 0, SPLITS[i])
+            elif k == "LS":
+                lace_part(("t", i), dz[i], "S", SPLITS[i], W)
+            elif k == "XV":
+                lace_part(("x", i), x_sb[i], "V", 0, XSPLITS[i])
+            elif k == "XS":
+                lace_part(("x", i), x_sb[i], "S", XSPLITS[i], W)
+            elif k == "QT":
+                dz_tok[i] = quantise(flat(laced[("t", i)]), E5M2, keep, "tok%d" % i)
+            elif k == "QU":
+                dz_unit[i] = quantise(turned[("t", i)][:], E5M2, keep, "unit%d" % i)
+            elif k == "IQ":
+                iw_codes[i] = quantise(turned[("w", i)][:], E4M3, keep, "iw%d" % i)
+            elif k == "XQ":
+                x_codes[i] = quantise(flat(laced[("x", i)]), E4M3, keep, "x%d" % i)
+            elif k == "M0":
+                products0(i, s[2])
+            elif k == "P1":
+                pass1(i, s[2], 0)
+            elif k == "M1":
+                if (i, s[2]) not in early:
+                    pass1(i, s[2], 0)
+                pass1(i, s[2], 1)
+            elif k == "C0":
+                copy0(i, s[2], s[3])
+            else:
+                copy1(i, s[2], s[3])

@@ -19,174 +19,188 @@ P = 128
 W = 512
 GROUPS = TOKENS // W
 CHUNKS = UNITS // W
-BLOCKS = [[0,0],[0,1],[1,0],[1,1],[0,3],[0,2],[1,2],[1,3]]
-SPLITS = [320,384,320,256,192,320,0,512]
-XSPLITS = [256,0]
-LOADS = [["b",0],["w",0],["b",2],["b",3],["x",1],["x",0],["b",1],["w",3],["w",1],["b",5],["b",4],["w",2],["b",6],["b",7]]
+BLOCKS = [[0,0],[0,1],[0,2],[0,3],[1,0],[1,1],[1,2],[1,3]]
+PARTS = [[[0,2],[2,4]],[[0,4]],[[0,2],[2,4]],[[0,2],[2,4]],[[0,4]],[[0,4]]]
+MEMBERS = [[0],[1],[2,3],[4,5],[6],[7]]
+SPLITS = [256,128,448,256,512,256,384,512]
+XSPLITS = [0,0]
+LOADS = [["S",0,0],["w",0],["S",0,1],["S",1,0],["S",2,0],["S",2,1],["w",1],["S",3,0],["x",1],["S",3,1],["x",0],["S",4,0],["S",5,0]]
 ORDER = [
     ["A",0,0],
     ["T",0,0],
-    ["A",0,1],
     ["E",0,0],
+    ["TI",0,0],
+    ["TI",0,1],
+    ["EI",0,0],
+    ["A",0,1],
+    ["TI",1,0],
+    ["EI",0,1],
+    ["IQ",0],
     ["LS",0],
     ["T",0,1],
     ["LV",0],
-    ["TI",0,0],
+    ["TI",1,1],
     ["E",0,1],
     ["QT",0],
-    ["TI",0,1],
-    ["EI",0,0],
-    ["QU",0],
-    ["EI",0,1],
-    ["IQ",0],
-    ["A",2,0],
-    ["M0",0,0],
-    ["A",2,1],
-    ["T",2,0],
-    ["E",2,0],
-    ["T",2,1],
-    ["LV",2],
-    ["LS",2],
-    ["A",3,0],
-    ["E",2,1],
-    ["QU",2],
-    ["XS",1],
-    ["T",3,0],
-    ["A",3,1],
-    ["XV",0],
-    ["T",3,1],
-    ["QT",2],
-    ["E",3,0],
-    ["XQ",1],
-    ["E",3,1],
-    ["LV",3],
-    ["LS",3],
-    ["QU",3],
-    ["A",1,0],
-    ["XS",0],
-    ["TI",3,0],
-    ["A",1,1],
-    ["T",1,0],
-    ["EI",3,0],
-    ["TI",1,0],
-    ["E",1,0],
-    ["XQ",0],
-    ["T",1,1],
     ["EI",1,0],
-    ["QT",3],
-    ["TI",1,1],
-    ["E",1,1],
-    ["LV",1],
-    ["TI",3,1],
+    ["QU",0],
     ["EI",1,1],
-    ["P1",0,0],
-    ["EI",3,1],
-    ["QU",1],
-    ["M1",0,0],
-    ["P1",0,1],
-    ["C1",0,0,"S"],
-    ["IQ",1],
-    ["M1",0,1],
-    ["P1",0,2],
-    ["C1",0,1,"S"],
-    ["A",5,0],
-    ["M1",0,2],
-    ["M0",0,1],
-    ["C1",0,2,"S"],
-    ["A",5,1],
+    ["A",1,0],
+    ["M0",0,0,0],
+    ["M0",0,0,1],
+    ["M0",0,0,2],
+    ["M0",0,0,3],
     ["LS",1],
-    ["T",5,0],
+    ["LV",1],
+    ["T",1,0],
+    ["T",1,1],
+    ["A",2,0],
+    ["E",1,0],
+    ["E",1,1],
     ["QT",1],
-    ["T",5,1],
-    ["E",5,0],
-    ["IQ",3],
-    ["P1",0,3],
-    ["E",5,1],
-    ["M1",0,3],
-    ["A",4,0],
-    ["LS",5],
-    ["P1",1,0],
-    ["M1",1,0],
-    ["P1",1,1],
-    ["M1",1,1],
-    ["C1",0,3,"S"],
-    ["C1",1,0,"V"],
+    ["T",2,0],
+    ["T",3,0],
+    ["E",2,0],
+    ["A",2,1],
+    ["E",3,0],
+    ["QU",1],
+    ["LS",2],
+    ["T",2,1],
+    ["LS",3],
+    ["IQ",1],
     ["TI",2,0],
-    ["C1",1,1,"S"],
-    ["A",4,1],
+    ["LV",2],
+    ["E",2,1],
     ["TI",2,1],
     ["EI",2,0],
-    ["T",4,0],
+    ["QT",2],
+    ["TI",3,0],
     ["EI",2,1],
-    ["QU",5],
-    ["T",4,1],
-    ["E",4,0],
+    ["QU",2],
     ["IQ",2],
-    ["P1",1,2],
-    ["E",4,1],
+    ["TI",3,1],
+    ["EI",3,0],
+    ["LV",3],
+    ["XS",1],
+    ["A",3,0],
+    ["T",3,1],
+    ["M0",0,1,0],
+    ["M0",0,1,1],
+    ["M0",0,1,2],
+    ["EI",3,1],
+    ["QT",3],
+    ["T",4,0],
+    ["E",3,1],
+    ["A",3,1],
+    ["M0",0,1,3],
+    ["E",4,0],
+    ["M0",0,2,0],
+    ["XS",0],
+    ["M0",0,2,1],
+    ["M0",0,2,2],
+    ["M0",0,2,3],
+    ["T",5,0],
+    ["QU",3],
+    ["T",4,1],
+    ["IQ",3],
+    ["T",5,1],
     ["LV",4],
-    ["M1",1,2],
-    ["M0",0,2],
-    ["C1",1,2,"S"],
-    ["QU",4],
-    ["LS",4],
-    ["A",6,0],
-    ["M0",0,3],
-    ["A",6,1],
-    ["T",6,0],
+    ["M0",0,3,0],
+    ["E",4,1],
+    ["M0",0,3,1],
+    ["M0",0,3,2],
     ["C0",0,0,"S"],
+    ["M0",0,3,3],
     ["C0",0,1,"S"],
-    ["C0",0,2,"V"],
-    ["T",6,1],
-    ["C0",0,3,"S"],
-    ["A",7,0],
-    ["P1",1,3],
-    ["E",6,0],
-    ["M1",1,3],
-    ["M0",1,0],
-    ["C1",1,3,"S"],
-    ["A",7,1],
-    ["E",6,1],
-    ["M0",1,1],
-    ["LS",6],
-    ["QU",6],
     ["QT",4],
-    ["M0",1,2],
+    ["C0",0,2,"S"],
+    ["QU",4],
+    ["C0",0,3,"S"],
+    ["XQ",0],
+    ["M0",1,0,0],
+    ["E",5,0],
+    ["M0",1,0,1],
+    ["XQ",1],
+    ["P1",0,0],
+    ["E",5,1],
+    ["P1",0,1],
     ["LV",5],
-    ["T",7,0],
+    ["P1",0,2],
+    ["LS",5],
+    ["P1",0,3],
+    ["M1",0,0],
+    ["A",4,0],
+    ["M1",0,1],
+    ["M1",0,2],
+    ["M1",0,3],
+    ["C1",0,0,"S"],
+    ["M0",1,0,2],
+    ["M0",1,0,3],
+    ["C1",0,1,"S"],
+    ["P1",1,0],
+    ["C1",0,2,"S"],
+    ["P1",1,1],
     ["QT",5],
+    ["C1",0,3,"S"],
+    ["P1",1,2],
+    ["QU",5],
+    ["M1",1,0],
+    ["LS",6],
+    ["P1",1,3],
+    ["LV",6],
+    ["M1",1,1],
+    ["M1",1,2],
+    ["C1",1,0,"S"],
+    ["M1",1,3],
+    ["C1",1,1,"S"],
+    ["M0",1,1,0],
+    ["A",5,0],
+    ["M0",1,1,1],
+    ["C1",1,2,"S"],
+    ["M0",1,1,2],
+    ["M0",1,1,3],
+    ["C1",1,3,"S"],
+    ["T",6,0],
+    ["T",6,1],
+    ["E",6,0],
+    ["E",6,1],
+    ["QT",6],
+    ["T",7,0],
     ["T",7,1],
     ["E",7,0],
-    ["QT",6],
-    ["P1",2,0],
+    ["QU",6],
+    ["M1",2,0],
     ["E",7,1],
     ["LV",7],
-    ["M1",2,0],
-    ["P1",2,1],
-    ["C1",2,0,"S"],
     ["M1",2,1],
-    ["P1",2,2],
-    ["C1",2,1,"S"],
-    ["QU",7],
+    ["C1",2,0,"S"],
     ["M1",2,2],
-    ["P1",2,3],
-    ["C1",2,2,"S"],
-    ["QT",7],
+    ["C1",2,1,"S"],
     ["M1",2,3],
-    ["M0",1,3],
+    ["QT",7],
+    ["C1",2,2,"S"],
+    ["M0",1,2,0],
     ["C1",2,3,"S"],
+    ["QU",7],
     ["M1",3,0],
-    ["C0",1,0,"V"],
-    ["C0",1,1,"S"],
     ["M1",3,1],
-    ["C0",1,2,"S"],
-    ["C0",1,3,"V"],
+    ["C1",3,0,"V"],
     ["M1",3,2],
-    ["C1",3,0,"S"],
     ["C1",3,1,"V"],
     ["M1",3,3],
     ["C1",3,2,"V"],
+    ["M0",1,2,1],
     ["C1",3,3,"V"],
+    ["M0",1,2,2],
+    ["M0",1,2,3],
+    ["M0",1,3,0],
+    ["M0",1,3,1],
+    ["C0",1,0,"V"],
+    ["M0",1,3,2],
+    ["C0",1,1,"S"],
+    ["M0",1,3,3],
+    ["C0",1,2,"V"],
+    ["C0",1,3,"S"],
 ]
 
 
@@ -196,14 +210,13 @@ def tile_eisnucell_pa_v_kernel(
     nc = tc.nc
     with ExitStack() as ctx:
         keep = ctx.enter_context(tc.tile_pool(name="keep", bufs=1))
-        zpool = ctx.enter_context(tc.tile_pool(name="zpool", bufs=5))
-        gpool = ctx.enter_context(tc.tile_pool(name="gpool", bufs=6))
-        rawpool = ctx.enter_context(tc.tile_pool(name="rawpool", bufs=6))
-        dzpool = ctx.enter_context(tc.tile_pool(name="dzpool", bufs=4))
+        zpool = ctx.enter_context(tc.tile_pool(name="zpool", bufs=3))
+        rawpool = ctx.enter_context(tc.tile_pool(name="rawpool", bufs=5))
+        dzpool = ctx.enter_context(tc.tile_pool(name="dzpool", bufs=3))
         lacepool = ctx.enter_context(tc.tile_pool(name="lacepool", bufs=4))
-        turnpool = ctx.enter_context(tc.tile_pool(name="turnpool", bufs=5))
-        out0pool = ctx.enter_context(tc.tile_pool(name="out0pool", bufs=2))
-        out1pool = ctx.enter_context(tc.tile_pool(name="out1pool", bufs=2))
+        turnpool = ctx.enter_context(tc.tile_pool(name="turnpool", bufs=4))
+        respool = ctx.enter_context(tc.tile_pool(name="respool", bufs=5))
+        unitpool = ctx.enter_context(tc.tile_pool(name="unitpool", bufs=5))
         psum = ctx.enter_context(tc.psum_pool(name="psum", bufs=4))
         psum_sum = ctx.enter_context(tc.psum_pool(name="psum_sum", bufs=1))
         ctx.enter_context(tc.manual_schedule())
@@ -214,67 +227,112 @@ def tile_eisnucell_pa_v_kernel(
         blocks = BLOCKS
         z_sb, g_sb, iw_sb, x_sb = {}, {}, {}, {}
 
-        def load_block(b, parts):
-            g, u = blocks[b]
+        def load_part(s, i):
+            g, u = blocks[MEMBERS[s][0]]
+            width = W * len(MEMBERS[s])
+            cols = slice(u * W % HALF, u * W % HALF + width)
             z_hbm, g_hbm = (z_exc, grad_0) if u < CHUNKS // 2 else (z_inh, grad_1)
             rows = slice(g * W, (g + 1) * W)
-            cols = slice(u * W % HALF, u * W % HALF + W)
-            g_view = g_hbm[rows, cols].rearrange("(p j) w -> p j w", j=4)
-            z_view = z_hbm[rows, cols].rearrange("(p j) w -> p j w", j=4)
-            gt = gpool.tile([P, 4, W], BF16, name="gt", tag="gt")
-            zt = zpool.tile([P, 4, W], F32, name="zt", tag="zt")
-            for i in range(parts):
-                js = slice(4 // parts * i, 4 // parts * (i + 1))
-                nc.sync.dma_start(out=gt[:, js, :], in_=g_view[:, js, :])
-                nc.sync.dma_start(out=zt[:, js, :], in_=z_view[:, js, :])
-            z_sb[b], g_sb[b] = zt, gt
+            if i == 0:
+                g_sb[s] = rawpool.tile([P, 4, width], BF16, name="raw", tag="raw")
+                z_sb[s] = zpool.tile([P, 4, width], F32, name="zt", tag="zt")
+            js = slice(PARTS[s][i][0], PARTS[s][i][1])
+            nc.sync.dma_start(out=g_sb[s][:, js, :], in_=g_hbm[rows, cols].rearrange("(p j) w -> p j w", j=4)[:, js, :])
+            nc.sync.dma_start(out=z_sb[s][:, js, :], in_=z_hbm[rows, cols].rearrange("(p j) w -> p j w", j=4)[:, js, :])
 
-        def load_iw(u):
-            t = rawpool.tile([P, 4, W], BF16, name="raw", tag="raw")
-            nc.sync.dma_start(out=t[:], in_=iw[:, u * W : (u + 1) * W].rearrange("(r p) k -> p r k", p=P))
-            iw_sb[u] = t
+        def load_iw(i):
+            t = rawpool.tile([P, 4, HALF], BF16, name="raw", tag="raw")
+            nc.sync.dma_start(out=t[:], in_=iw[:, i * HALF : (i + 1) * HALF].rearrange("(r p) k -> p r k", p=P))
+            iw_sb[i] = t
 
         def load_x(g):
             t = rawpool.tile([P, 4, W], BF16, name="raw", tag="raw")
             nc.sync.dma_start(out=t[:], in_=x_t[g * W : (g + 1) * W, :].rearrange("(p j) w -> p j w", j=4))
             x_sb[g] = t
 
-        for kind, i in LOADS:
-            if kind == "b":
-                load_block(i, 2 if i == 0 else 1)
-            elif kind == "w":
-                load_iw(i)
+        for ld in LOADS:
+            if ld[0] == "S":
+                load_part(ld[1], ld[2])
+            elif ld[0] == "w":
+                load_iw(ld[1])
             else:
-                load_x(i)
+                load_x(ld[1])
 
-        sc, ve = nc.scalar.copy, nc.vector.tensor_copy
+        at = {tuple(blk): b for b, blk in enumerate(blocks)}
+        unit = {b: (s, i) for s, members in enumerate(MEMBERS) for i, b in enumerate(members)}
+        dz, laced, turned, banks = {}, {}, {}, {}
+        dz_tok, dz_unit, iw_codes, x_codes, sums, res0, res1 = {}, {}, {}, {}, {}, {}, {}
+        copy = {"V": nc.vector.tensor_copy, "S": nc.scalar.copy}
 
-        def lace(engine_copy, dst, src, c0, c1):
-            engine_copy(
-                out=dst[:, c0:c1, :].rearrange("p (c i) t -> p c t i", i=4),
-                in_=src[:, :, c0:c1].rearrange("p t (c i) -> p c t i", i=4),
+        def mask(s, i):
+            if i == 0:
+                dz[s] = dzpool.tile([P, 2, 4, P * len(MEMBERS[s]), 2], BF16, name="dz", tag="dz")
+            j0, j1 = PARTS[s][i]
+            for u in range(2):
+                nc.vector.scalar_tensor_tensor(
+                    out=dz[s][:, u, j0:j1, :, :].rearrange("p j n e -> p (j n) e"),
+                    in0=z_sb[s][:, j0:j1, :].rearrange("p j (n v) -> p (j n) v", v=4)[:, :, 2 * u : 2 * u + 2],
+                    scalar=0.0,
+                    in1=g_sb[s][:, j0:j1, :].rearrange("p j (n v) -> p (j n) v", v=4)[:, :, 2 * u : 2 * u + 2],
+                    op0=ALU.is_gt,
+                    op1=ALU.mult,
+                )
+
+        def lace_dz(b, e, c0, c1):
+            key = ("t", b)
+            if key not in laced:
+                laced[key] = lacepool.tile([P, W, 4], BF16, name="laced", tag="laced", align_bytes=64)
+            n0 = unit[b][1] * P
+            for u in range(2):
+                copy[e](
+                    out=laced[key][:, c0:c1, :].rearrange("p (n u e) t -> p u n t e", u=2, e=2)[:, u],
+                    in_=dz[unit[b][0]][:, u, :, n0 + c0 // 4 : n0 + c1 // 4, :].rearrange("p t n e -> p n t e"),
+                )
+
+        def lace_x(g, e, c0, c1):
+            key = ("x", g)
+            if key not in laced:
+                laced[key] = lacepool.tile([P, W, 4], BF16, name="laced", tag="laced", align_bytes=64)
+            copy[e](
+                out=laced[key][:, c0:c1, :].rearrange("p (c i) t -> p c t i", i=4),
+                in_=x_sb[g][:, :, c0:c1].rearrange("p t (c i) -> p c t i", i=4),
             )
 
-        def turn(src, h):
-            words = src[:].rearrange("p j w -> p (j w)").bitcast(F32)
+        def turn_dz(b, h):
+            s, i = unit[b]
+            words = dz[s][:].rearrange("p u j n e -> p (u j n e)").bitcast(F32)
             bank = psum.tile([P, 2, 2, P], F32, name="bank", tag="bank")
             for jj in range(2):
-                for e in range(2):
-                    j = 2 * h + jj
-                    nc.tensor.transpose(bank[:, jj, e, :], words[:, 256 * j + e : 256 * (j + 1) : 2], ident[:])
+                for u in range(2):
+                    w0 = ((u * 4 + 2 * h + jj) * len(MEMBERS[s]) + i) * P
+                    nc.tensor.transpose(bank[:, jj, u, :], words[:, w0 : w0 + P], ident[:])
             return bank
 
-        def unload_turn(bank, dst, h):
+        def turn_iw(i, h):
+            words = iw_sb[i // 2][:].rearrange("p r k -> p (r k)").bitcast(F32)
+            bank = psum.tile([P, 2, 2, P], F32, name="bank", tag="bank")
+            for jj in range(2):
+                for u in range(2):
+                    w0 = (2 * h + jj) * 512 + i % 2 * 256 + u
+                    nc.tensor.transpose(bank[:, jj, u, :], words[:, w0 : w0 + 255 : 2], ident[:])
+            return bank
+
+        def unload(key, h):
+            if key not in turned:
+                turned[key] = turnpool.tile([P, 4 * W], BF16, name="turned", tag="turned", align_bytes=64)
             nc.scalar.copy(
-                out=dst[:].bitcast(F32)[:, 512 * h : 512 * (h + 1)].rearrange("p (j q u) -> p j q u", j=2, u=2),
-                in_=bank[:].rearrange("p j u q -> p j q u"),
+                out=turned[key][:].bitcast(F32)[:, 512 * h : 512 * (h + 1)].rearrange("p (j q u) -> p j q u", j=2, u=2),
+                in_=banks[key + (h,)][:].rearrange("p j u q -> p j q u"),
             )
 
-        def quantise(src2d, fmt, pool, tag):
+        def quantise(src2d, fmt, tag, pool):
             codes = pool.tile([P, W], U32, name=tag + "_c", tag=tag + "_c", align_bytes=64)
             scales = pool.tile([P, W], U8, name=tag + "_s", tag=tag + "_s", align_bytes=64)
             nc.vector.quantize_mx(out=codes[:].bitcast(fmt), scales=scales[:], in_=src2d)
             return codes, scales
+
+        def flat(t):
+            return t[:].rearrange("p w t -> p (w t)")
 
         def mm(out, left, lfmt, lcols, right, rfmt, start, stop):
             nc.tensor.matmul_mx(
@@ -287,40 +345,13 @@ def tile_eisnucell_pa_v_kernel(
                 stop=stop,
             )
 
-        def flat(t):
-            return t[:].rearrange("p w t -> p (w t)")
-
-        at = {tuple(blk): b for b, blk in enumerate(blocks)}
-        dz, laced, turned, banks = {}, {}, {}, {}
-        dz_tok, dz_unit, iw_codes, x_codes, sums, res0, res1 = {}, {}, {}, {}, {}, {}, {}
-        copy = {"V": nc.vector.tensor_copy, "S": nc.scalar.copy}
-
-        def mask(b, h):
-            if h == 0:
-                dz[b] = dzpool.tile([P, 4, W], BF16, name="dz", tag="dz")
-            js = slice(2 * h, 2 * h + 2)
-            nc.vector.scalar_tensor_tensor(
-                out=dz[b][:, js, :], in0=z_sb[b][:, js, :], scalar=0.0, in1=g_sb[b][:, js, :], op0=ALU.is_gt, op1=ALU.mult
+        def products0(g, u, j):
+            if u == 0:
+                sums[(g, j)] = psum_sum.tile([P, W], F32, name="sum0_%d" % j, tag="sum0_%d" % j)
+            mm(
+                sums[(g, j)][:], dz_unit[at[(g, u)]], E5M2, slice(P * j, P * (j + 1)), iw_codes[u], E4M3,
+                u == 0, u == CHUNKS - 1,
             )
-
-        def lace_part(key, src, e, c0, c1):
-            if key not in laced:
-                laced[key] = lacepool.tile([P, W, 4], BF16, name="laced", tag="laced", align_bytes=64)
-            lace(copy[e], laced[key], src, c0, c1)
-
-        def unload(key, h):
-            if key not in turned:
-                turned[key] = turnpool.tile([P, 4 * W], BF16, name="turned", tag="turned", align_bytes=64)
-            unload_turn(banks[key + (h,)], turned[key], h)
-
-        def products0(g, u):
-            for j in range(4):
-                if u == 0:
-                    sums[(g, j)] = psum_sum.tile([P, W], F32, name="sum0_%d" % j, tag="sum0_%d" % j)
-                mm(
-                    sums[(g, j)][:], dz_unit[at[(g, u)]], E5M2, slice(P * j, P * (j + 1)), iw_codes[u], E4M3,
-                    u == 0, u == CHUNKS - 1,
-                )
 
         def pass1(u, m, g):
             if g == 0:
@@ -341,12 +372,12 @@ def tile_eisnucell_pa_v_kernel(
 
         def copy0(g, j, e):
             if g not in res0:
-                res0[g] = out0pool.tile([P, 4, W], F32, name="res0", tag="res0")
+                res0[g] = respool.tile([P, 4, W], F32, name="res", tag="res")
             store(res0[g], out_0[g * W : (g + 1) * W, :].rearrange("(p j) n -> p j n", j=4), (0, g), j, e, sums[(g, j)])
 
         def copy1(u, m, e):
             if u not in res1:
-                res1[u] = out1pool.tile([P, 4, W], F32, name="res1", tag="res1")
+                res1[u] = respool.tile([P, 4, W], F32, name="res", tag="res")
             store(res1[u], out_1[:, u * W : (u + 1) * W].rearrange("(m p) n -> p m n", p=P), (1, u), m, e, banks[("m", u, m)])
 
         early = {(s[1], s[2]) for s in ORDER if s[0] == "P1"}
@@ -355,31 +386,31 @@ def tile_eisnucell_pa_v_kernel(
             if k == "A":
                 mask(i, s[2])
             elif k == "T":
-                banks[("t", i, s[2])] = turn(dz[i], s[2])
+                banks[("t", i, s[2])] = turn_dz(i, s[2])
             elif k == "E":
                 unload(("t", i), s[2])
             elif k == "TI":
-                banks[("w", i, s[2])] = turn(iw_sb[i], s[2])
+                banks[("w", i, s[2])] = turn_iw(i, s[2])
             elif k == "EI":
                 unload(("w", i), s[2])
             elif k == "LV":
-                lace_part(("t", i), dz[i], "V", 0, SPLITS[i])
+                lace_dz(i, "V", 0, SPLITS[i])
             elif k == "LS":
-                lace_part(("t", i), dz[i], "S", SPLITS[i], W)
+                lace_dz(i, "S", SPLITS[i], W)
             elif k == "XV":
-                lace_part(("x", i), x_sb[i], "V", 0, XSPLITS[i])
+                lace_x(i, "V", 0, XSPLITS[i])
             elif k == "XS":
-                lace_part(("x", i), x_sb[i], "S", XSPLITS[i], W)
+                lace_x(i, "S", XSPLITS[i], W)
             elif k == "QT":
-                dz_tok[i] = quantise(flat(laced[("t", i)]), E5M2, keep, "tok%d" % i)
+                dz_tok[i] = quantise(flat(laced[("t", i)]), E5M2, "tok%d" % i, keep)
             elif k == "QU":
-                dz_unit[i] = quantise(turned[("t", i)][:], E5M2, keep, "unit%d" % i)
+                dz_unit[i] = quantise(turned[("t", i)][:], E5M2, "unit", unitpool)
             elif k == "IQ":
-                iw_codes[i] = quantise(turned[("w", i)][:], E4M3, keep, "iw%d" % i)
+                iw_codes[i] = quantise(turned[("w", i)][:], E4M3, "iw%d" % i, keep)
             elif k == "XQ":
-                x_codes[i] = quantise(flat(laced[("x", i)]), E4M3, keep, "x%d" % i)
+                x_codes[i] = quantise(flat(laced[("x", i)]), E4M3, "x%d" % i, keep)
             elif k == "M0":
-                products0(i, s[2])
+                products0(i, s[2], s[3])
             elif k == "P1":
                 pass1(i, s[2], 0)
             elif k == "M1":

@@ -19,188 +19,195 @@ P = 128
 W = 512
 GROUPS = TOKENS // W
 CHUNKS = UNITS // W
-BLOCKS = [[0,0],[0,1],[0,2],[0,3],[1,0],[1,1],[1,2],[1,3]]
-PARTS = [[[0,2],[2,4]],[[0,4]],[[0,2],[2,4]],[[0,2],[2,4]],[[0,4]],[[0,4]]]
+BLOCKS = [[0,0],[0,1],[1,0],[1,1],[0,2],[0,3],[1,2],[1,3]]
+PARTS = [[[0,1],[1,2],[2,4]],[[0,4]],[[0,2],[2,4]],[[0,2],[2,4]],[[0,4]],[[0,4]]]
 MEMBERS = [[0],[1],[2,3],[4,5],[6],[7]]
-SPLITS = [256,128,448,256,512,256,384,512]
-XSPLITS = [0,0]
-LOADS = [["S",0,0],["w",0],["S",0,1],["S",1,0],["S",2,0],["S",2,1],["w",1],["S",3,0],["x",1],["S",3,1],["x",0],["S",4,0],["S",5,0]]
+SPLITS = [512,64,0,192,0,512,512,512]
+XSPLITS = [320,0]
+SLOTS = {"z": ["z0","z1","z2","z1","z2","z0"], "g": ["e0","e1","e2","e0","e1","e3"], "dz": ["d0","d1","d2","d1","d0","d2"], "w": ["e4","e3"], "x": ["e1","e2"], "lt": ["f6","f0","f5","f4","f4","f1","f6","f5"], "lx": ["f5","f6"], "tt": ["f0","f1","f3","f2","f5","f2","f0","f3"], "tw": ["f3","f0","f1","f3"]}
+LOADS = [["S",0,0],["S",1,0],["S",2,1],["S",2,0],["S",0,1],["S",0,2],["w",1,0],["w",0,0],["x",0,0],["x",1,0],["S",3,1],["S",3,0],["S",4,0],["S",5,0]]
 ORDER = [
-    ["A",0,0],
-    ["T",0,0],
-    ["E",0,0],
-    ["TI",0,0],
-    ["TI",0,1],
-    ["EI",0,0],
-    ["A",0,1],
-    ["TI",1,0],
-    ["EI",0,1],
-    ["IQ",0],
-    ["LS",0],
-    ["T",0,1],
-    ["LV",0],
-    ["TI",1,1],
-    ["E",0,1],
-    ["QT",0],
-    ["EI",1,0],
-    ["QU",0],
-    ["EI",1,1],
-    ["A",1,0],
-    ["M0",0,0,0],
-    ["M0",0,0,1],
-    ["M0",0,0,2],
-    ["M0",0,0,3],
-    ["LS",1],
-    ["LV",1],
-    ["T",1,0],
-    ["T",1,1],
-    ["A",2,0],
-    ["E",1,0],
-    ["E",1,1],
-    ["QT",1],
-    ["T",2,0],
-    ["T",3,0],
-    ["E",2,0],
-    ["A",2,1],
-    ["E",3,0],
-    ["QU",1],
-    ["LS",2],
-    ["T",2,1],
-    ["LS",3],
-    ["IQ",1],
-    ["TI",2,0],
-    ["LV",2],
-    ["E",2,1],
-    ["TI",2,1],
-    ["EI",2,0],
-    ["QT",2],
-    ["TI",3,0],
-    ["EI",2,1],
-    ["QU",2],
-    ["IQ",2],
-    ["TI",3,1],
-    ["EI",3,0],
-    ["LV",3],
-    ["XS",1],
-    ["A",3,0],
-    ["T",3,1],
-    ["M0",0,1,0],
-    ["M0",0,1,1],
-    ["M0",0,1,2],
-    ["EI",3,1],
-    ["QT",3],
-    ["T",4,0],
-    ["E",3,1],
-    ["A",3,1],
-    ["M0",0,1,3],
-    ["E",4,0],
-    ["M0",0,2,0],
-    ["XS",0],
-    ["M0",0,2,1],
-    ["M0",0,2,2],
-    ["M0",0,2,3],
-    ["T",5,0],
-    ["QU",3],
-    ["T",4,1],
-    ["IQ",3],
-    ["T",5,1],
-    ["LV",4],
-    ["M0",0,3,0],
-    ["E",4,1],
-    ["M0",0,3,1],
-    ["M0",0,3,2],
-    ["C0",0,0,"S"],
-    ["M0",0,3,3],
-    ["C0",0,1,"S"],
-    ["QT",4],
-    ["C0",0,2,"S"],
-    ["QU",4],
-    ["C0",0,3,"S"],
-    ["XQ",0],
-    ["M0",1,0,0],
-    ["E",5,0],
-    ["M0",1,0,1],
-    ["XQ",1],
-    ["P1",0,0],
-    ["E",5,1],
-    ["P1",0,1],
-    ["LV",5],
-    ["P1",0,2],
-    ["LS",5],
-    ["P1",0,3],
-    ["M1",0,0],
-    ["A",4,0],
-    ["M1",0,1],
-    ["M1",0,2],
-    ["M1",0,3],
-    ["C1",0,0,"S"],
-    ["M0",1,0,2],
-    ["M0",1,0,3],
-    ["C1",0,1,"S"],
-    ["P1",1,0],
-    ["C1",0,2,"S"],
-    ["P1",1,1],
-    ["QT",5],
-    ["C1",0,3,"S"],
-    ["P1",1,2],
-    ["QU",5],
-    ["M1",1,0],
-    ["LS",6],
-    ["P1",1,3],
-    ["LV",6],
-    ["M1",1,1],
-    ["M1",1,2],
-    ["C1",1,0,"S"],
-    ["M1",1,3],
-    ["C1",1,1,"S"],
-    ["M0",1,1,0],
-    ["A",5,0],
-    ["M0",1,1,1],
-    ["C1",1,2,"S"],
-    ["M0",1,1,2],
-    ["M0",1,1,3],
-    ["C1",1,3,"S"],
-    ["T",6,0],
-    ["T",6,1],
-    ["E",6,0],
-    ["E",6,1],
-    ["QT",6],
-    ["T",7,0],
-    ["T",7,1],
-    ["E",7,0],
-    ["QU",6],
-    ["M1",2,0],
-    ["E",7,1],
-    ["LV",7],
-    ["M1",2,1],
-    ["C1",2,0,"S"],
-    ["M1",2,2],
-    ["C1",2,1,"S"],
-    ["M1",2,3],
-    ["QT",7],
-    ["C1",2,2,"S"],
-    ["M0",1,2,0],
-    ["C1",2,3,"S"],
-    ["QU",7],
-    ["M1",3,0],
-    ["M1",3,1],
-    ["C1",3,0,"V"],
-    ["M1",3,2],
-    ["C1",3,1,"V"],
-    ["M1",3,3],
-    ["C1",3,2,"V"],
-    ["M0",1,2,1],
-    ["C1",3,3,"V"],
-    ["M0",1,2,2],
-    ["M0",1,2,3],
-    ["M0",1,3,0],
-    ["M0",1,3,1],
-    ["C0",1,0,"V"],
-    ["M0",1,3,2],
-    ["C0",1,1,"S"],
-    ["M0",1,3,3],
-    ["C0",1,2,"V"],
-    ["C0",1,3,"S"],
+    ["A",0,0,0,"V"],
+    ["A",1,0,0,"V"],
+    ["T",1,1,0,"T"],
+    ["LV",1,0,0,"V"],
+    ["T",1,0,0,"T"],
+    ["E",1,1,0,"S"],
+    ["A",2,1,0,"V"],
+    ["LS",1,0,0,"S"],
+    ["E",1,0,0,"V"],
+    ["T",3,1,0,"T"],
+    ["QT",1,0,0,"V"],
+    ["T",2,1,0,"T"],
+    ["E",3,1,0,"S"],
+    ["A",2,0,0,"V"],
+    ["E",2,1,0,"S"],
+    ["A",0,1,0,"V"],
+    ["LS",3,0,0,"S"],
+    ["T",3,0,0,"T"],
+    ["A",0,2,0,"V"],
+    ["T",2,0,0,"T"],
+    ["E",2,0,0,"S"],
+    ["E",3,0,0,"V"],
+    ["T",0,1,0,"T"],
+    ["LS",2,0,0,"S"],
+    ["QU",2,0,0,"V"],
+    ["T",0,0,0,"T"],
+    ["QU",1,0,0,"V"],
+    ["TI",0,1,0,"T"],
+    ["LV",0,0,0,"V"],
+    ["TI",2,1,0,"T"],
+    ["E",0,1,0,"S"],
+    ["LV",3,0,0,"V"],
+    ["E",0,0,0,"S"],
+    ["QT",2,0,0,"V"],
+    ["TI",0,0,0,"T"],
+    ["EI",0,1,0,"S"],
+    ["QT",0,0,0,"V"],
+    ["EI",2,1,0,"S"],
+    ["TI",1,0,0,"T"],
+    ["QU",0,0,0,"V"],
+    ["EI",0,0,0,"S"],
+    ["XV",0,0,0,"V"],
+    ["XS",0,0,0,"S"],
+    ["TI",1,1,0,"T"],
+    ["IQ",0,0,0,"V"],
+    ["XS",1,0,0,"S"],
+    ["QU",3,0,0,"V"],
+    ["M0",0,0,2,"T"],
+    ["EI",1,0,0,"V"],
+    ["M0",0,0,0,"T"],
+    ["XQ",0,0,0,"V"],
+    ["TI",3,1,0,"T"],
+    ["QT",3,0,0,"V"],
+    ["EI",1,1,0,"S"],
+    ["P1",0,0,0,"T"],
+    ["XQ",1,0,0,"V"],
+    ["P1",0,3,0,"T"],
+    ["EI",3,1,0,"S"],
+    ["IQ",1,0,0,"V"],
+    ["P1",1,1,0,"T"],
+    ["M1",0,0,0,"T"],
+    ["A",3,1,0,"V"],
+    ["M1",1,1,0,"T"],
+    ["C1",0,0,0,"S"],
+    ["P1",1,0,0,"T"],
+    ["M1",0,3,0,"T"],
+    ["C1",1,1,0,"S"],
+    ["M0",0,0,3,"T"],
+    ["M0",0,0,1,"T"],
+    ["C1",0,3,0,"S"],
+    ["M1",1,0,0,"T"],
+    ["TI",3,0,0,"T"],
+    ["C1",1,0,0,"S"],
+    ["A",3,0,0,"V"],
+    ["T",5,1,0,"T"],
+    ["EI",3,0,0,"S"],
+    ["TI",2,0,0,"T"],
+    ["E",5,1,0,"S"],
+    ["M0",0,1,3,"T"],
+    ["M0",0,1,2,"T"],
+    ["EI",2,0,0,"S"],
+    ["T",4,1,0,"T"],
+    ["IQ",3,0,0,"V"],
+    ["T",4,0,0,"T"],
+    ["E",4,1,0,"S"],
+    ["T",5,0,0,"T"],
+    ["IQ",2,0,0,"V"],
+    ["E",4,0,0,"S"],
+    ["M0",0,1,0,"T"],
+    ["E",5,0,0,"V"],
+    ["M0",0,1,1,"T"],
+    ["LS",4,0,0,"S"],
+    ["P1",1,3,0,"T"],
+    ["QU",4,0,0,"V"],
+    ["P1",0,2,0,"T"],
+    ["M1",1,3,0,"T"],
+    ["QU",5,0,0,"V"],
+    ["P1",0,1,0,"T"],
+    ["M0",0,2,0,"T"],
+    ["P1",1,2,0,"T"],
+    ["A",4,0,0,"V"],
+    ["M0",0,2,3,"T"],
+    ["M1",1,2,0,"T"],
+    ["M0",0,3,3,"T"],
+    ["C1",1,3,0,"S"],
+    ["M0",0,3,0,"T"],
+    ["M1",0,1,0,"T"],
+    ["C0",0,3,0,"S"],
+    ["M1",0,2,0,"T"],
+    ["M0",0,2,1,"T"],
+    ["C1",0,1,0,"S"],
+    ["QT",4,0,0,"V"],
+    ["M0",1,0,3,"T"],
+    ["M0",0,3,1,"T"],
+    ["C0",0,0,0,"S"],
+    ["M0",0,2,2,"T"],
+    ["A",5,0,0,"V"],
+    ["M0",0,3,2,"T"],
+    ["C0",0,1,0,"S"],
+    ["M0",1,1,3,"T"],
+    ["T",6,1,0,"T"],
+    ["C0",0,2,0,"S"],
+    ["M0",1,0,1,"T"],
+    ["C1",0,2,0,"S"],
+    ["M0",1,1,1,"T"],
+    ["M0",1,0,0,"T"],
+    ["C1",1,2,0,"S"],
+    ["LV",6,0,0,"V"],
+    ["T",6,0,0,"T"],
+    ["E",6,1,0,"S"],
+    ["T",7,0,0,"T"],
+    ["T",7,1,0,"T"],
+    ["E",6,0,0,"S"],
+    ["P1",2,2,0,"T"],
+    ["E",7,1,0,"S"],
+    ["QT",6,0,0,"V"],
+    ["M0",1,1,0,"T"],
+    ["P1",2,3,0,"T"],
+    ["E",7,0,0,"S"],
+    ["QU",6,0,0,"V"],
+    ["M1",2,2,0,"T"],
+    ["M1",2,3,0,"T"],
+    ["QU",7,0,0,"V"],
+    ["C1",2,2,0,"S"],
+    ["P1",2,1,0,"T"],
+    ["P1",2,0,0,"T"],
+    ["LV",5,0,0,"V"],
+    ["C1",2,3,0,"S"],
+    ["M1",2,1,0,"T"],
+    ["M1",2,0,0,"T"],
+    ["C1",2,1,0,"S"],
+    ["M0",1,2,0,"T"],
+    ["M0",1,2,1,"T"],
+    ["C1",2,0,0,"S"],
+    ["M0",1,3,0,"T"],
+    ["LV",7,0,0,"V"],
+    ["M0",1,3,1,"T"],
+    ["C0",1,0,0,"S"],
+    ["M0",1,0,2,"T"],
+    ["M0",1,2,3,"T"],
+    ["C0",1,1,0,"S"],
+    ["M0",1,1,2,"T"],
+    ["M0",1,3,3,"T"],
+    ["QT",5,0,0,"V"],
+    ["M0",1,2,2,"T"],
+    ["C0",1,3,0,"S"],
+    ["M0",1,3,2,"T"],
+    ["QT",7,0,0,"V"],
+    ["P1",3,1,0,"T"],
+    ["C0",1,2,0,"S"],
+    ["P1",3,0,0,"T"],
+    ["M1",3,1,0,"T"],
+    ["M1",3,0,0,"T"],
+    ["C1",3,1,0,"V"],
+    ["P1",3,3,0,"T"],
+    ["C1",3,0,0,"S"],
+    ["P1",3,2,0,"T"],
+    ["M1",3,3,0,"T"],
+    ["M1",3,2,0,"T"],
+    ["C1",3,3,0,"V"],
+    ["C1",3,2,0,"S"],
 ]
 
 
@@ -210,13 +217,7 @@ def tile_eisnucell_pa_v_kernel(
     nc = tc.nc
     with ExitStack() as ctx:
         keep = ctx.enter_context(tc.tile_pool(name="keep", bufs=1))
-        zpool = ctx.enter_context(tc.tile_pool(name="zpool", bufs=3))
-        rawpool = ctx.enter_context(tc.tile_pool(name="rawpool", bufs=5))
-        dzpool = ctx.enter_context(tc.tile_pool(name="dzpool", bufs=3))
-        lacepool = ctx.enter_context(tc.tile_pool(name="lacepool", bufs=4))
-        turnpool = ctx.enter_context(tc.tile_pool(name="turnpool", bufs=4))
-        respool = ctx.enter_context(tc.tile_pool(name="respool", bufs=5))
-        unitpool = ctx.enter_context(tc.tile_pool(name="unitpool", bufs=5))
+        big = ctx.enter_context(tc.tile_pool(name="big", bufs=1))
         psum = ctx.enter_context(tc.psum_pool(name="psum", bufs=4))
         psum_sum = ctx.enter_context(tc.psum_pool(name="psum_sum", bufs=1))
         ctx.enter_context(tc.manual_schedule())
@@ -233,20 +234,20 @@ def tile_eisnucell_pa_v_kernel(
             cols = slice(u * W % HALF, u * W % HALF + width)
             z_hbm, g_hbm = (z_exc, grad_0) if u < CHUNKS // 2 else (z_inh, grad_1)
             rows = slice(g * W, (g + 1) * W)
-            if i == 0:
-                g_sb[s] = rawpool.tile([P, 4, width], BF16, name="raw", tag="raw")
-                z_sb[s] = zpool.tile([P, 4, width], F32, name="zt", tag="zt")
+            if s not in g_sb:
+                g_sb[s] = big.tile([P, 4, width], BF16, name=SLOTS["g"][s], tag=SLOTS["g"][s], align_bytes=64)
+                z_sb[s] = big.tile([P, 4, width], F32, name=SLOTS["z"][s], tag=SLOTS["z"][s], align_bytes=64)
             js = slice(PARTS[s][i][0], PARTS[s][i][1])
             nc.sync.dma_start(out=g_sb[s][:, js, :], in_=g_hbm[rows, cols].rearrange("(p j) w -> p j w", j=4)[:, js, :])
             nc.sync.dma_start(out=z_sb[s][:, js, :], in_=z_hbm[rows, cols].rearrange("(p j) w -> p j w", j=4)[:, js, :])
 
-        def load_iw(i):
-            t = rawpool.tile([P, 4, HALF], BF16, name="raw", tag="raw")
-            nc.sync.dma_start(out=t[:], in_=iw[:, i * HALF : (i + 1) * HALF].rearrange("(r p) k -> p r k", p=P))
-            iw_sb[i] = t
+        def load_iw(h):
+            t = big.tile([P, 2, UNITS], BF16, name=SLOTS["w"][h], tag=SLOTS["w"][h], align_bytes=64)
+            nc.sync.dma_start(out=t[:], in_=iw[2 * P * h : 2 * P * (h + 1), :].rearrange("(r p) k -> p r k", p=P))
+            iw_sb[h] = t
 
         def load_x(g):
-            t = rawpool.tile([P, 4, W], BF16, name="raw", tag="raw")
+            t = big.tile([P, 4, W], BF16, name=SLOTS["x"][g], tag=SLOTS["x"][g], align_bytes=64)
             nc.sync.dma_start(out=t[:], in_=x_t[g * W : (g + 1) * W, :].rearrange("(p j) w -> p j w", j=4))
             x_sb[g] = t
 
@@ -265,8 +266,8 @@ def tile_eisnucell_pa_v_kernel(
         copy = {"V": nc.vector.tensor_copy, "S": nc.scalar.copy}
 
         def mask(s, i):
-            if i == 0:
-                dz[s] = dzpool.tile([P, 2, 4, P * len(MEMBERS[s]), 2], BF16, name="dz", tag="dz")
+            if s not in dz:
+                dz[s] = big.tile([P, 2, 4, P * len(MEMBERS[s]), 2], BF16, name=SLOTS["dz"][s], tag=SLOTS["dz"][s], align_bytes=64)
             j0, j1 = PARTS[s][i]
             for u in range(2):
                 nc.vector.scalar_tensor_tensor(
@@ -281,7 +282,7 @@ def tile_eisnucell_pa_v_kernel(
         def lace_dz(b, e, c0, c1):
             key = ("t", b)
             if key not in laced:
-                laced[key] = lacepool.tile([P, W, 4], BF16, name="laced", tag="laced", align_bytes=64)
+                laced[key] = big.tile([P, W, 4], BF16, name=SLOTS["lt"][b], tag=SLOTS["lt"][b], align_bytes=64)
             n0 = unit[b][1] * P
             for u in range(2):
                 copy[e](
@@ -292,7 +293,7 @@ def tile_eisnucell_pa_v_kernel(
         def lace_x(g, e, c0, c1):
             key = ("x", g)
             if key not in laced:
-                laced[key] = lacepool.tile([P, W, 4], BF16, name="laced", tag="laced", align_bytes=64)
+                laced[key] = big.tile([P, W, 4], BF16, name=SLOTS["lx"][g], tag=SLOTS["lx"][g], align_bytes=64)
             copy[e](
                 out=laced[key][:, c0:c1, :].rearrange("p (c i) t -> p c t i", i=4),
                 in_=x_sb[g][:, :, c0:c1].rearrange("p t (c i) -> p c t i", i=4),
@@ -309,18 +310,18 @@ def tile_eisnucell_pa_v_kernel(
             return bank
 
         def turn_iw(i, h):
-            words = iw_sb[i // 2][:].rearrange("p r k -> p (r k)").bitcast(F32)
+            words = iw_sb[h][:].rearrange("p r k -> p (r k)").bitcast(F32)
             bank = psum.tile([P, 2, 2, P], F32, name="bank", tag="bank")
             for jj in range(2):
                 for u in range(2):
-                    w0 = (2 * h + jj) * 512 + i % 2 * 256 + u
+                    w0 = jj * (UNITS // 2) + i * 256 + u
                     nc.tensor.transpose(bank[:, jj, u, :], words[:, w0 : w0 + 255 : 2], ident[:])
             return bank
 
-        def unload(key, h):
+        def unload(key, h, e):
             if key not in turned:
-                turned[key] = turnpool.tile([P, 4 * W], BF16, name="turned", tag="turned", align_bytes=64)
-            nc.scalar.copy(
+                turned[key] = big.tile([P, 4 * W], BF16, name=SLOTS["t" + key[0]][key[1]], tag=SLOTS["t" + key[0]][key[1]], align_bytes=64)
+            copy[e](
                 out=turned[key][:].bitcast(F32)[:, 512 * h : 512 * (h + 1)].rearrange("p (j q u) -> p j q u", j=2, u=2),
                 in_=banks[key + (h,)][:].rearrange("p j u q -> p j q u"),
             )
@@ -363,24 +364,31 @@ def tile_eisnucell_pa_v_kernel(
 
         done = set()
 
-        def store(res, view, key, j, e, src):
-            copy[e](out=res[:, j, :], in_=src[:])
-            done.add(key + (j,))
-            if key + (j ^ 1,) in done:
-                js = slice(j // 2 * 2, j // 2 * 2 + 2)
-                nc.sync.dma_start(out=view[:, js, :], in_=res[:, js, :])
-
         def copy0(g, j, e):
             if g not in res0:
-                res0[g] = respool.tile([P, 4, W], F32, name="res", tag="res")
-            store(res0[g], out_0[g * W : (g + 1) * W, :].rearrange("(p j) n -> p j n", j=4), (0, g), j, e, sums[(g, j)])
+                res0[g] = keep.tile([P, 4, W], F32, name="res0_%d" % g, tag="res0_%d" % g)
+            copy[e](out=res0[g][:, j, :], in_=sums[(g, j)][:])
+            done.add((0, g, j))
+            if (0, g, j ^ 1) in done:
+                js = slice(j // 2 * 2, j // 2 * 2 + 2)
+                view = out_0[g * W : (g + 1) * W, :].rearrange("(p j) n -> p j n", j=4)
+                nc.sync.dma_start(out=view[:, js, :], in_=res0[g][:, js, :])
 
         def copy1(u, m, e):
-            if u not in res1:
-                res1[u] = respool.tile([P, 4, W], F32, name="res", tag="res")
-            store(res1[u], out_1[:, u * W : (u + 1) * W].rearrange("(m p) n -> p m n", p=P), (1, u), m, e, banks[("m", u, m)])
+            i = u // 2
+            if i not in res1:
+                res1[i] = keep.tile([P, 4, HALF], F32, name="res1_%d" % i, tag="res1_%d" % i)
+            cols = slice(u % 2 * W, u % 2 * W + W)
+            copy[e](out=res1[i][:, m, cols], in_=banks[("m", u, m)][:])
+            done.add((1, u, m))
+            if i == 0:
+                if (1, u ^ 1, m) in done:
+                    nc.sync.dma_start(out=out_1[P * m : P * (m + 1), 0:HALF], in_=res1[i][:, m, :])
+            elif (1, u, m ^ 1) in done:
+                ms = slice(m // 2 * 2, m // 2 * 2 + 2)
+                view = out_1[:, u * W : (u + 1) * W].rearrange("(m p) n -> p m n", p=P)
+                nc.sync.dma_start(out=view[:, ms, :], in_=res1[i][:, ms, cols])
 
-        early = {(s[1], s[2]) for s in ORDER if s[0] == "P1"}
         for s in ORDER:
             k, i = s[0], s[1]
             if k == "A":
@@ -388,11 +396,11 @@ def tile_eisnucell_pa_v_kernel(
             elif k == "T":
                 banks[("t", i, s[2])] = turn_dz(i, s[2])
             elif k == "E":
-                unload(("t", i), s[2])
+                unload(("t", i), s[2], s[4])
             elif k == "TI":
                 banks[("w", i, s[2])] = turn_iw(i, s[2])
             elif k == "EI":
-                unload(("w", i), s[2])
+                unload(("w", i), s[2], s[4])
             elif k == "LV":
                 lace_dz(i, "V", 0, SPLITS[i])
             elif k == "LS":
@@ -404,7 +412,7 @@ def tile_eisnucell_pa_v_kernel(
             elif k == "QT":
                 dz_tok[i] = quantise(flat(laced[("t", i)]), E5M2, "tok%d" % i, keep)
             elif k == "QU":
-                dz_unit[i] = quantise(turned[("t", i)][:], E5M2, "unit", unitpool)
+                dz_unit[i] = quantise(turned[("t", i)][:], E5M2, "unit%d" % i, keep)
             elif k == "IQ":
                 iw_codes[i] = quantise(turned[("w", i)][:], E4M3, "iw%d" % i, keep)
             elif k == "XQ":
@@ -414,10 +422,8 @@ def tile_eisnucell_pa_v_kernel(
             elif k == "P1":
                 pass1(i, s[2], 0)
             elif k == "M1":
-                if (i, s[2]) not in early:
-                    pass1(i, s[2], 0)
                 pass1(i, s[2], 1)
             elif k == "C0":
-                copy0(i, s[2], s[3])
+                copy0(i, s[2], s[4])
             else:
-                copy1(i, s[2], s[3])
+                copy1(i, s[2], s[4])

from contextlib import ExitStack

import concourse.mybir as mybir
from concourse.masks import make_identity

TOKENS, N_IN, UNITS, HALF = 1024, 512, 2048, 1024
FLOPS = 2 * (2 * TOKENS * UNITS * N_IN)
BYTES = 2 * TOKENS * N_IN + 2 * N_IN * UNITS + 6 * TOKENS * UNITS + 4 * TOKENS * N_IN + 4 * N_IN * UNITS

F32 = mybir.dt.float32
BF16 = mybir.dt.bfloat16
U32 = mybir.dt.uint32
U8 = mybir.dt.uint8
E4M3 = mybir.dt.float8_e4m3fn_x4
E5M2 = mybir.dt.float8_e5m2_x4
ALU = mybir.AluOpType

P = 128
W = 512
GROUPS = TOKENS // W
CHUNKS = UNITS // W
BLOCKS = [[0,0],[0,1],[1,0],[1,1],[0,2],[0,3],[1,2],[1,3]]
PARTS = [[[0,1],[1,2],[2,4]],[[0,4]],[[0,2],[2,4]],[[0,2],[2,4]],[[0,4]],[[0,4]]]
MEMBERS = [[0],[1],[2,3],[4,5],[6],[7]]
SPLITS = [512,64,0,192,0,512,512,512]
XSPLITS = [320,0]
SLOTS = {"z": ["z0","z1","z2","z1","z2","z0"], "g": ["e0","e1","e2","e0","e1","e3"], "dz": ["d0","d1","d2","d1","d0","d2"], "w": ["e4","e3"], "x": ["e1","e2"], "lt": ["f6","f0","f5","f4","f4","f1","f6","f5"], "lx": ["f5","f6"], "tt": ["f0","f1","f3","f2","f5","f2","f0","f3"], "tw": ["f3","f0","f1","f3"]}
LOADS = [["S",0,0],["S",1,0],["S",2,1],["S",2,0],["S",0,1],["S",0,2],["w",1,0],["w",0,0],["x",0,0],["x",1,0],["S",3,1],["S",3,0],["S",4,0],["S",5,0]]
ORDER = [
    ["A",0,0,0,"V"],
    ["A",1,0,0,"V"],
    ["T",1,1,0,"T"],
    ["LV",1,0,0,"V"],
    ["T",1,0,0,"T"],
    ["E",1,1,0,"S"],
    ["A",2,1,0,"V"],
    ["LS",1,0,0,"S"],
    ["E",1,0,0,"V"],
    ["T",3,1,0,"T"],
    ["QT",1,0,0,"V"],
    ["T",2,1,0,"T"],
    ["E",3,1,0,"S"],
    ["A",2,0,0,"V"],
    ["E",2,1,0,"S"],
    ["A",0,1,0,"V"],
    ["LS",3,0,0,"S"],
    ["T",3,0,0,"T"],
    ["A",0,2,0,"V"],
    ["T",2,0,0,"T"],
    ["E",2,0,0,"S"],
    ["E",3,0,0,"V"],
    ["T",0,1,0,"T"],
    ["LS",2,0,0,"S"],
    ["QU",2,0,0,"V"],
    ["T",0,0,0,"T"],
    ["QU",1,0,0,"V"],
    ["TI",0,1,0,"T"],
    ["LV",0,0,0,"V"],
    ["TI",2,1,0,"T"],
    ["E",0,1,0,"S"],
    ["LV",3,0,0,"V"],
    ["E",0,0,0,"S"],
    ["QT",2,0,0,"V"],
    ["TI",0,0,0,"T"],
    ["EI",0,1,0,"S"],
    ["QT",0,0,0,"V"],
    ["EI",2,1,0,"S"],
    ["TI",1,0,0,"T"],
    ["QU",0,0,0,"V"],
    ["EI",0,0,0,"S"],
    ["XV",0,0,0,"V"],
    ["XS",0,0,0,"S"],
    ["TI",1,1,0,"T"],
    ["IQ",0,0,0,"V"],
    ["XS",1,0,0,"S"],
    ["QU",3,0,0,"V"],
    ["M0",0,0,2,"T"],
    ["EI",1,0,0,"V"],
    ["M0",0,0,0,"T"],
    ["XQ",0,0,0,"V"],
    ["TI",3,1,0,"T"],
    ["QT",3,0,0,"V"],
    ["EI",1,1,0,"S"],
    ["P1",0,0,0,"T"],
    ["XQ",1,0,0,"V"],
    ["P1",0,3,0,"T"],
    ["EI",3,1,0,"S"],
    ["IQ",1,0,0,"V"],
    ["P1",1,1,0,"T"],
    ["M1",0,0,0,"T"],
    ["A",3,1,0,"V"],
    ["M1",1,1,0,"T"],
    ["C1",0,0,0,"S"],
    ["P1",1,0,0,"T"],
    ["M1",0,3,0,"T"],
    ["C1",1,1,0,"S"],
    ["M0",0,0,3,"T"],
    ["M0",0,0,1,"T"],
    ["C1",0,3,0,"S"],
    ["M1",1,0,0,"T"],
    ["TI",3,0,0,"T"],
    ["C1",1,0,0,"S"],
    ["A",3,0,0,"V"],
    ["T",5,1,0,"T"],
    ["EI",3,0,0,"S"],
    ["TI",2,0,0,"T"],
    ["E",5,1,0,"S"],
    ["M0",0,1,3,"T"],
    ["M0",0,1,2,"T"],
    ["EI",2,0,0,"S"],
    ["T",4,1,0,"T"],
    ["IQ",3,0,0,"V"],
    ["T",4,0,0,"T"],
    ["E",4,1,0,"S"],
    ["T",5,0,0,"T"],
    ["IQ",2,0,0,"V"],
    ["E",4,0,0,"S"],
    ["M0",0,1,0,"T"],
    ["E",5,0,0,"V"],
    ["M0",0,1,1,"T"],
    ["LS",4,0,0,"S"],
    ["P1",1,3,0,"T"],
    ["QU",4,0,0,"V"],
    ["P1",0,2,0,"T"],
    ["M1",1,3,0,"T"],
    ["QU",5,0,0,"V"],
    ["P1",0,1,0,"T"],
    ["M0",0,2,0,"T"],
    ["P1",1,2,0,"T"],
    ["A",4,0,0,"V"],
    ["M0",0,2,3,"T"],
    ["M1",1,2,0,"T"],
    ["M0",0,3,3,"T"],
    ["C1",1,3,0,"S"],
    ["M0",0,3,0,"T"],
    ["M1",0,1,0,"T"],
    ["C0",0,3,0,"S"],
    ["M1",0,2,0,"T"],
    ["M0",0,2,1,"T"],
    ["C1",0,1,0,"S"],
    ["QT",4,0,0,"V"],
    ["M0",1,0,3,"T"],
    ["M0",0,3,1,"T"],
    ["C0",0,0,0,"S"],
    ["M0",0,2,2,"T"],
    ["A",5,0,0,"V"],
    ["M0",0,3,2,"T"],
    ["C0",0,1,0,"S"],
    ["M0",1,1,3,"T"],
    ["T",6,1,0,"T"],
    ["C0",0,2,0,"S"],
    ["M0",1,0,1,"T"],
    ["C1",0,2,0,"S"],
    ["M0",1,1,1,"T"],
    ["M0",1,0,0,"T"],
    ["C1",1,2,0,"S"],
    ["LV",6,0,0,"V"],
    ["T",6,0,0,"T"],
    ["E",6,1,0,"S"],
    ["T",7,0,0,"T"],
    ["T",7,1,0,"T"],
    ["E",6,0,0,"S"],
    ["P1",2,2,0,"T"],
    ["E",7,1,0,"S"],
    ["QT",6,0,0,"V"],
    ["M0",1,1,0,"T"],
    ["P1",2,3,0,"T"],
    ["E",7,0,0,"S"],
    ["QU",6,0,0,"V"],
    ["M1",2,2,0,"T"],
    ["M1",2,3,0,"T"],
    ["QU",7,0,0,"V"],
    ["C1",2,2,0,"S"],
    ["P1",2,1,0,"T"],
    ["P1",2,0,0,"T"],
    ["LV",5,0,0,"V"],
    ["C1",2,3,0,"S"],
    ["M1",2,1,0,"T"],
    ["M1",2,0,0,"T"],
    ["C1",2,1,0,"S"],
    ["M0",1,2,0,"T"],
    ["M0",1,2,1,"T"],
    ["C1",2,0,0,"S"],
    ["M0",1,3,0,"T"],
    ["LV",7,0,0,"V"],
    ["M0",1,3,1,"T"],
    ["C0",1,0,0,"S"],
    ["M0",1,0,2,"T"],
    ["M0",1,2,3,"T"],
    ["C0",1,1,0,"S"],
    ["M0",1,1,2,"T"],
    ["M0",1,3,3,"T"],
    ["QT",5,0,0,"V"],
    ["M0",1,2,2,"T"],
    ["C0",1,3,0,"S"],
    ["M0",1,3,2,"T"],
    ["QT",7,0,0,"V"],
    ["P1",3,1,0,"T"],
    ["C0",1,2,0,"S"],
    ["P1",3,0,0,"T"],
    ["M1",3,1,0,"T"],
    ["M1",3,0,0,"T"],
    ["C1",3,1,0,"V"],
    ["P1",3,3,0,"T"],
    ["C1",3,0,0,"S"],
    ["P1",3,2,0,"T"],
    ["M1",3,3,0,"T"],
    ["M1",3,2,0,"T"],
    ["C1",3,3,0,"V"],
    ["C1",3,2,0,"S"],
]


def tile_eisnucell_pa_v_kernel(
    tc, x_t, y_exc, s_exc, y_inh, s_inh, iw, eiw, l, z_exc, z_inh, grad_0, grad_1, out_0, out_1
):
    nc = tc.nc
    with ExitStack() as ctx:
        keep = ctx.enter_context(tc.tile_pool(name="keep", bufs=1))
        big = ctx.enter_context(tc.tile_pool(name="big", bufs=1))
        psum = ctx.enter_context(tc.psum_pool(name="psum", bufs=4))
        psum_sum = ctx.enter_context(tc.psum_pool(name="psum_sum", bufs=1))
        ctx.enter_context(tc.manual_schedule())

        ident = keep.tile([P, P], F32, name="ident")
        make_identity(nc, ident[:])

        blocks = BLOCKS
        z_sb, g_sb, iw_sb, x_sb = {}, {}, {}, {}

        def load_part(s, i):
            g, u = blocks[MEMBERS[s][0]]
            width = W * len(MEMBERS[s])
            cols = slice(u * W % HALF, u * W % HALF + width)
            z_hbm, g_hbm = (z_exc, grad_0) if u < CHUNKS // 2 else (z_inh, grad_1)
            rows = slice(g * W, (g + 1) * W)
            if s not in g_sb:
                g_sb[s] = big.tile([P, 4, width], BF16, name=SLOTS["g"][s], tag=SLOTS["g"][s], align_bytes=64)
                z_sb[s] = big.tile([P, 4, width], F32, name=SLOTS["z"][s], tag=SLOTS["z"][s], align_bytes=64)
            js = slice(PARTS[s][i][0], PARTS[s][i][1])
            nc.sync.dma_start(out=g_sb[s][:, js, :], in_=g_hbm[rows, cols].rearrange("(p j) w -> p j w", j=4)[:, js, :])
            nc.sync.dma_start(out=z_sb[s][:, js, :], in_=z_hbm[rows, cols].rearrange("(p j) w -> p j w", j=4)[:, js, :])

        def load_iw(h):
            t = big.tile([P, 2, UNITS], BF16, name=SLOTS["w"][h], tag=SLOTS["w"][h], align_bytes=64)
            nc.sync.dma_start(out=t[:], in_=iw[2 * P * h : 2 * P * (h + 1), :].rearrange("(r p) k -> p r k", p=P))
            iw_sb[h] = t

        def load_x(g):
            t = big.tile([P, 4, W], BF16, name=SLOTS["x"][g], tag=SLOTS["x"][g], align_bytes=64)
            nc.sync.dma_start(out=t[:], in_=x_t[g * W : (g + 1) * W, :].rearrange("(p j) w -> p j w", j=4))
            x_sb[g] = t

        for ld in LOADS:
            if ld[0] == "S":
                load_part(ld[1], ld[2])
            elif ld[0] == "w":
                load_iw(ld[1])
            else:
                load_x(ld[1])

        at = {tuple(blk): b for b, blk in enumerate(blocks)}
        unit = {b: (s, i) for s, members in enumerate(MEMBERS) for i, b in enumerate(members)}
        dz, laced, turned, banks = {}, {}, {}, {}
        dz_tok, dz_unit, iw_codes, x_codes, sums, res0, res1 = {}, {}, {}, {}, {}, {}, {}
        copy = {"V": nc.vector.tensor_copy, "S": nc.scalar.copy}

        def mask(s, i):
            if s not in dz:
                dz[s] = big.tile([P, 2, 4, P * len(MEMBERS[s]), 2], BF16, name=SLOTS["dz"][s], tag=SLOTS["dz"][s], align_bytes=64)
            j0, j1 = PARTS[s][i]
            for u in range(2):
                nc.vector.scalar_tensor_tensor(
                    out=dz[s][:, u, j0:j1, :, :].rearrange("p j n e -> p (j n) e"),
                    in0=z_sb[s][:, j0:j1, :].rearrange("p j (n v) -> p (j n) v", v=4)[:, :, 2 * u : 2 * u + 2],
                    scalar=0.0,
                    in1=g_sb[s][:, j0:j1, :].rearrange("p j (n v) -> p (j n) v", v=4)[:, :, 2 * u : 2 * u + 2],
                    op0=ALU.is_gt,
                    op1=ALU.mult,
                )

        def lace_dz(b, e, c0, c1):
            key = ("t", b)
            if key not in laced:
                laced[key] = big.tile([P, W, 4], BF16, name=SLOTS["lt"][b], tag=SLOTS["lt"][b], align_bytes=64)
            n0 = unit[b][1] * P
            for u in range(2):
                copy[e](
                    out=laced[key][:, c0:c1, :].rearrange("p (n u e) t -> p u n t e", u=2, e=2)[:, u],
                    in_=dz[unit[b][0]][:, u, :, n0 + c0 // 4 : n0 + c1 // 4, :].rearrange("p t n e -> p n t e"),
                )

        def lace_x(g, e, c0, c1):
            key = ("x", g)
            if key not in laced:
                laced[key] = big.tile([P, W, 4], BF16, name=SLOTS["lx"][g], tag=SLOTS["lx"][g], align_bytes=64)
            copy[e](
                out=laced[key][:, c0:c1, :].rearrange("p (c i) t -> p c t i", i=4),
                in_=x_sb[g][:, :, c0:c1].rearrange("p t (c i) -> p c t i", i=4),
            )

        def turn_dz(b, h):
            s, i = unit[b]
            words = dz[s][:].rearrange("p u j n e -> p (u j n e)").bitcast(F32)
            bank = psum.tile([P, 2, 2, P], F32, name="bank", tag="bank")
            for jj in range(2):
                for u in range(2):
                    w0 = ((u * 4 + 2 * h + jj) * len(MEMBERS[s]) + i) * P
                    nc.tensor.transpose(bank[:, jj, u, :], words[:, w0 : w0 + P], ident[:])
            return bank

        def turn_iw(i, h):
            words = iw_sb[h][:].rearrange("p r k -> p (r k)").bitcast(F32)
            bank = psum.tile([P, 2, 2, P], F32, name="bank", tag="bank")
            for jj in range(2):
                for u in range(2):
                    w0 = jj * (UNITS // 2) + i * 256 + u
                    nc.tensor.transpose(bank[:, jj, u, :], words[:, w0 : w0 + 255 : 2], ident[:])
            return bank

        def unload(key, h, e):
            if key not in turned:
                turned[key] = big.tile([P, 4 * W], BF16, name=SLOTS["t" + key[0]][key[1]], tag=SLOTS["t" + key[0]][key[1]], align_bytes=64)
            copy[e](
                out=turned[key][:].bitcast(F32)[:, 512 * h : 512 * (h + 1)].rearrange("p (j q u) -> p j q u", j=2, u=2),
                in_=banks[key + (h,)][:].rearrange("p j u q -> p j q u"),
            )

        def quantise(src2d, fmt, tag, pool):
            codes = pool.tile([P, W], U32, name=tag + "_c", tag=tag + "_c", align_bytes=64)
            scales = pool.tile([P, W], U8, name=tag + "_s", tag=tag + "_s", align_bytes=64)
            nc.vector.quantize_mx(out=codes[:].bitcast(fmt), scales=scales[:], in_=src2d)
            return codes, scales

        def flat(t):
            return t[:].rearrange("p w t -> p (w t)")

        def mm(out, left, lfmt, lcols, right, rfmt, start, stop):
            nc.tensor.matmul_mx(
                out=out,
                lhsT=left[0][:, lcols].bitcast(lfmt),
                lhsT_scale=left[1][:, lcols],
                rhs=right[0][:].bitcast(rfmt),
                rhs_scale=right[1][:],
                start=start,
                stop=stop,
            )

        def products0(g, u, j):
            if u == 0:
                sums[(g, j)] = psum_sum.tile([P, W], F32, name="sum0_%d" % j, tag="sum0_%d" % j)
            mm(
                sums[(g, j)][:], dz_unit[at[(g, u)]], E5M2, slice(P * j, P * (j + 1)), iw_codes[u], E4M3,
                u == 0, u == CHUNKS - 1,
            )

        def pass1(u, m, g):
            if g == 0:
                banks[("m", u, m)] = psum.tile([P, W], F32, name="bank", tag="bank")
            mm(
                banks[("m", u, m)][:], x_codes[g], E4M3, slice(P * m, P * (m + 1)), dz_tok[at[(g, u)]], E5M2,
                g == 0, g == GROUPS - 1,
            )

        done = set()

        def copy0(g, j, e):
            if g not in res0:
                res0[g] = keep.tile([P, 4, W], F32, name="res0_%d" % g, tag="res0_%d" % g)
            copy[e](out=res0[g][:, j, :], in_=sums[(g, j)][:])
            done.add((0, g, j))
            if (0, g, j ^ 1) in done:
                js = slice(j // 2 * 2, j // 2 * 2 + 2)
                view = out_0[g * W : (g + 1) * W, :].rearrange("(p j) n -> p j n", j=4)
                nc.sync.dma_start(out=view[:, js, :], in_=res0[g][:, js, :])

        def copy1(u, m, e):
            i = u // 2
            if i not in res1:
                res1[i] = keep.tile([P, 4, HALF], F32, name="res1_%d" % i, tag="res1_%d" % i)
            cols = slice(u % 2 * W, u % 2 * W + W)
            copy[e](out=res1[i][:, m, cols], in_=banks[("m", u, m)][:])
            done.add((1, u, m))
            if i == 0:
                if (1, u ^ 1, m) in done:
                    nc.sync.dma_start(out=out_1[P * m : P * (m + 1), 0:HALF], in_=res1[i][:, m, :])
            elif (1, u, m ^ 1) in done:
                ms = slice(m // 2 * 2, m // 2 * 2 + 2)
                view = out_1[:, u * W : (u + 1) * W].rearrange("(m p) n -> p m n", p=P)
                nc.sync.dma_start(out=view[:, ms, :], in_=res1[i][:, ms, cols])

        for s in ORDER:
            k, i = s[0], s[1]
            if k == "A":
                mask(i, s[2])
            elif k == "T":
                banks[("t", i, s[2])] = turn_dz(i, s[2])
            elif k == "E":
                unload(("t", i), s[2], s[4])
            elif k == "TI":
                banks[("w", i, s[2])] = turn_iw(i, s[2])
            elif k == "EI":
                unload(("w", i), s[2], s[4])
            elif k == "LV":
                lace_dz(i, "V", 0, SPLITS[i])
            elif k == "LS":
                lace_dz(i, "S", SPLITS[i], W)
            elif k == "XV":
                lace_x(i, "V", 0, XSPLITS[i])
            elif k == "XS":
                lace_x(i, "S", XSPLITS[i], W)
            elif k == "QT":
                dz_tok[i] = quantise(flat(laced[("t", i)]), E5M2, "tok%d" % i, keep)
            elif k == "QU":
                dz_unit[i] = quantise(turned[("t", i)][:], E5M2, "unit%d" % i, keep)
            elif k == "IQ":
                iw_codes[i] = quantise(turned[("w", i)][:], E4M3, "iw%d" % i, keep)
            elif k == "XQ":
                x_codes[i] = quantise(flat(laced[("x", i)]), E4M3, "x%d" % i, keep)
            elif k == "M0":
                products0(i, s[2], s[3])
            elif k == "P1":
                pass1(i, s[2], 0)
            elif k == "M1":
                pass1(i, s[2], 1)
            elif k == "C0":
                copy0(i, s[2], s[4])
            else:
                copy1(i, s[2], s[4])
